import numpy as np
import ml_dtypes


def mxq(x, axis, fmt="e4m3"):
    dtype, down = {"e4m3": (ml_dtypes.float8_e4m3fn, 7), "e5m2": (ml_dtypes.float8_e5m2, 14)}[fmt]
    v = np.moveaxis(np.asarray(x, np.float32).astype(ml_dtypes.bfloat16).astype(np.float64), axis, -1)
    blocks = v.reshape(v.shape[:-1] + (-1, 32))
    amax = np.abs(blocks).max(-1, keepdims=True)
    byte = np.maximum(np.where(amax > 0, np.frexp(amax)[1] - 1 + 127, 0) - down, 1)
    scale = np.exp2(byte - 127.0)
    codes = (blocks / scale).astype(np.float32).astype(dtype).astype(np.float64)
    return np.moveaxis((codes * scale).reshape(v.shape), -1, axis)


WIDE = False


def mx_kscale(k):
    if not WIDE:
        return np.ones(k)
    levels = np.array([10, -10, 5, -5, 0])
    if k % 512:
        return np.exp2(np.random.permutation(np.resize(levels, k // 32))).repeat(32)
    a = np.empty((k // 512, 16))
    for p in range(k // 512):
        a[p, :8] = np.random.permutation(np.resize(levels, 8))
        for g in range(8):
            far = levels[np.abs(levels - a[p, g]) >= 10]
            a[p, g + 8] = far[np.random.randint(len(far))]
    return np.exp2(a.ravel()).repeat(32)


BF16 = ml_dtypes.bfloat16


def bf(x):
    return np.asarray(x, np.float32).astype(BF16)


def f64(x):
    return np.asarray(x).astype(np.float64)


B, S, D, R, C = 128, 32, 512, 16, 1024
MIN_SCALE = 1e-3
TEMPERATURE = 1.5


def softplus(v):
    return np.logaddexp(v, 0.0)


def setup_inputs():
    s = mx_kscale(D)
    return {
        "features": bf(np.random.standard_normal((B, D)) * 0.3 * s),
        "W_diag": bf(np.random.standard_normal((D, D)) * 2.0 / np.sqrt(D) / s[None, :]),
        "b_diag": bf(-4.0 + 0.2 * np.random.standard_normal(D)),
        "W_cls": bf(np.random.standard_normal((C, D)) * 3.0 / np.sqrt(D) / s[None, :]),
        "b_cls": bf(np.random.standard_normal(C) * 0.3),
        "noise_diag": bf(np.random.standard_normal((B, S, D)) * 10.0 * s),
        "lr_samples": bf(np.random.standard_normal((B, S, D)) * 0.3 * s),
    }


def reference(features, W_diag, b_diag, W_cls, b_cls, noise_diag, lr_samples):
    f = f64(features)
    z = (mxq(f, 1, "e4m3") @ mxq(f64(W_diag), 1, "e4m3").T) + f64(b_diag)
    diagonal_std = softplus(z) + MIN_SCALE
    samples = f64(lr_samples) + diagonal_std[:, None, :] * f64(noise_diag)
    pre_logits = f[:, None, :] + samples
    logits = (mxq(pre_logits, 2, "e4m3") @ mxq(f64(W_cls), 1, "e4m3").T) + f64(b_cls)
    return logits / TEMPERATURE

@@ -1,0 +1,286 @@
+from contextlib import ExitStack
+
+import concourse.mybir as mybir
+from concourse.masks import make_identity
+
+F32 = mybir.dt.float32
+BF16 = mybir.dt.bfloat16
+U32 = mybir.dt.uint32
+U8 = mybir.dt.uint8
+FP8X4 = mybir.dt.float8_e4m3fn_x4
+ALU = mybir.AluOpType
+ACT = mybir.ActivationFunctionType
+
+B, S, D, C = 128, 32, 512, 1024
+P = 128
+FLOPS = 2 * B * S * D * C + 2 * B * D * D
+ZBANK = F32
+NG = 16
+GB = 8
+INV_T = 1.0 / 1.5
+LOADS = (("n", 0, 2), ("n", 2, 2), ("w", 0, 0), ("l", 0, 2), ("n", 4, 4), ("l", 2, 2), ("n", 8, 4), ("l", 4, 4), ("n", 12, 4), ("l", 8, 4), ("l", 12, 4))
+HEAD_NOISE = 8
+
+
+def tile_hetxlhead_pa_kernel(tc, features, W_diag, b_diag, W_cls, b_cls, noise_diag, lr_samples, out):
+    nc = tc.nc
+    with ExitStack() as ctx:
+        keep = ctx.enter_context(tc.tile_pool(name="keep", bufs=1))
+        work = ctx.enter_context(tc.tile_pool(name="work", bufs=3))
+        psum = ctx.enter_context(tc.psum_pool(name="psum", bufs=2))
+
+        n_rows = noise_diag.rearrange("b s d -> (b s) d").rearrange("(j r g) d -> r j g d", r=P, g=2)
+        l_rows = lr_samples.rearrange("b s d -> (b s) d").rearrange("(j r g) d -> r j g d", r=P, g=2)
+        o_rows = out.rearrange("b s c -> (b s) c").rearrange("(j r g) c -> r j g c", r=P, g=2)
+
+        f_raw = keep.tile([P, D], BF16, name="f_raw")
+        nc.sync.dma_start(out=f_raw[:], in_=features)
+        wd_rows = W_diag.rearrange("(m t) k -> m t k", t=4)
+        wd_raw = []
+        for i in range(2):
+            wd_half = keep.tile([P, 2, D], BF16, name="wd_raw%d" % i)
+            nc.sync.dma_start(out=wd_half[:], in_=wd_rows[:, 2 * i : 2 * i + 2])
+            wd_raw.append(wd_half)
+        bd = keep.tile([P, 4], BF16, name="bd")
+        nc.sync.dma_start(out=bd[:], in_=b_diag.rearrange("(p t) -> p t", t=4))
+
+        brow = keep.tile([P, C], BF16, name="brow")
+        nc.gpsimd.memset(brow[:], 0.0)
+        wc_raw = keep.tile([P, 8, D], BF16, name="wc_raw")
+
+        n_words = {}
+        l_words = {}
+        for li, (what, j0, n) in enumerate(LOADS):
+            if what == "w":
+                nc.sync.dma_start(out=wc_raw[:], in_=W_cls.rearrange("(a p) d -> p a d", p=P))
+                nc.sync.dma_start(out=brow[0:1, :], in_=b_cls.rearrange("(o c) -> o c", o=1))
+            else:
+                raw = keep.tile([P, n, 2, D], BF16, name="raw%d" % li)
+                rows = n_rows if what == "n" else l_rows
+                nc.sync.dma_start(out=raw[:], in_=rows[:, j0 : j0 + n])
+                for i in range(n):
+                    if what == "n":
+                        n_words[j0 + i] = raw[:, i].bitcast(F32)
+                    else:
+                        l_words[j0 + i] = raw[:, i].bitcast(F32)
+
+        ident = keep.tile([P, P], F32, name="ident")
+        make_identity(nc, ident[:])
+        ones = keep.tile([P, P], BF16, name="ones")
+        nc.gpsimd.memset(ones[:], 1.0)
+        warm = keep.tile([P, 2], F32, name="warm")
+        nc.vector.memset(warm[:], 0.0)
+        nc.scalar.activation(out=warm[:, 1:2], in_=warm[:, 0:1], func=ACT.Exp)
+
+        def transpose_words(dst, words):
+            for u in range(2):
+                nc.tensor.transpose(out=dst[:, u, :], in_=words[:, u : 256 : 2], identity=ident[:])
+
+        xf = psum.tile([P, 2, 2, P], F32, name="xf", tag="tA")
+        transpose_words(xf[:, 0], f_raw[:].bitcast(F32))
+        fg = keep.tile([P, B, 4], BF16, name="fg", align_bytes=64)
+        nc.vector.tensor_copy(out=fg[:].bitcast(F32), in_=xf[:, 0].rearrange("p u b -> p b u"))
+        f_codes = keep.tile([P, B], U32, name="f_codes", align_bytes=64)
+        f_scl = keep.tile([P, B], U8, name="f_scl", align_bytes=64)
+
+        nc.vector.quantize_mx(out=f_codes[:].bitcast(FP8X4), scales=f_scl[:], in_=fg[:].rearrange("p b t -> p (b t)"))
+        wd_codes = keep.tile([P, 4 * P], U32, name="wd_codes", align_bytes=64)
+        wd_scl = keep.tile([P, 4 * P], U8, name="wd_scl", align_bytes=64)
+        wdg = []
+        for i in range(2):
+            xw = psum.tile([P, 2, 2, P], F32, name="xw%d" % i, tag="tB")
+            wd_words = wd_raw[i][:].bitcast(F32)
+            for a in range(2):
+                transpose_words(xw[:, a], wd_words[:, a])
+            wdg_half = keep.tile([P, 2, P, 4], BF16, name="wdg%d" % i, align_bytes=64)
+            wdg.append(wdg_half)
+            src = xw[:].rearrange("p a u m -> p a m u")
+            if i == 0:
+                nc.vector.tensor_copy(out=wdg_half[:].bitcast(F32), in_=src)
+            else:
+                nc.scalar.copy(out=wdg_half[:].bitcast(F32), in_=src)
+        for i in range(2):
+            cols = slice(2 * i * P, (2 * i + 2) * P)
+            nc.vector.quantize_mx(
+                out=wd_codes[:, cols].bitcast(FP8X4), scales=wd_scl[:, cols], in_=wdg[i][:].rearrange("p t m k -> p (t m k)")
+            )
+
+        zt = psum.tile([P, 4, P], ZBANK, name="zt", tag="tA")
+        for t in range(4):
+            cols = slice(t * P, (t + 1) * P)
+            nc.tensor.matmul_mx(
+                out=zt[:, t, :],
+                lhsT=wd_codes[:, cols].bitcast(FP8X4),
+                lhsT_scale=wd_scl[:, cols],
+                rhs=f_codes[:].bitcast(FP8X4),
+                rhs_scale=f_scl[:],
+                start=True,
+                stop=True,
+            )
+
+        v = keep.tile([P, 4, B], F32, name="v")
+        nc.vector.tensor_tensor(out=v[:], in0=zt[:], in1=bd[:].unsqueeze(2).to_broadcast([P, 4, B]), op=ALU.add)
+        va = keep.tile([P, 4, B], F32, name="va")
+        nc.scalar.activation(out=va[:], in_=v[:], func=ACT.Abs)
+        ve = keep.tile([P, 4, B], F32, name="ve")
+        nc.scalar.activation(out=ve[:], in_=va[:], func=ACT.Exp, scale=-1.0)
+        vr = keep.tile([P, 4, B], F32, name="vr")
+        nc.vector.tensor_scalar(out=vr[:], in0=v[:], scalar1=0.0, scalar2=1e-3, op0=ALU.max, op1=ALU.add)
+        vl = keep.tile([P, 4, B], F32, name="vl")
+        std = keep.tile([P, 4, B], F32, name="std")
+        for b0, b1 in ((0, 32), (32, B)):
+            nc.scalar.activation(out=vl[:, :, b0:b1], in_=ve[:, :, b0:b1], func=ACT.Ln, bias=1.0)
+            nc.vector.tensor_tensor(out=std[:, :, b0:b1], in0=vr[:, :, b0:b1], in1=vl[:, :, b0:b1], op=ALU.add)
+
+        wc_words = wc_raw[:].bitcast(F32)
+        wcg = keep.tile([P, 8, P, 4], BF16, name="wcg", align_bytes=64)
+        wc_codes = keep.tile([P, C], U32, name="wc_codes", align_bytes=64)
+        wc_scl = keep.tile([P, C], U8, name="wc_scl", align_bytes=64)
+        for i in range(4):
+            xc = psum.tile([P, 2, 2, P], F32, name="xc%d" % i, tag="o", bufs=4)
+            for a in range(2):
+                transpose_words(xc[:, a], wc_words[:, 2 * i + a])
+            dst = wcg[:, 2 * i : 2 * i + 2].bitcast(F32)
+            src = xc[:].rearrange("p a u m -> p a m u")
+            if i % 2 == 0:
+                nc.vector.tensor_copy(out=dst, in_=src)
+            else:
+                nc.scalar.copy(out=dst, in_=src)
+        for h in range(2):
+            nc.vector.quantize_mx(
+                out=wc_codes[:, h * 512 : (h + 1) * 512].bitcast(FP8X4),
+                scales=wc_scl[:, h * 512 : (h + 1) * 512],
+                in_=wcg[:, 4 * h : 4 * h + 4].rearrange("p a m k -> p (a m k)"),
+            )
+        b15 = keep.tile([P, C], F32, name="b15")
+        for h in range(2):
+            pb = psum.tile([P, 512], F32, name="pb%d" % h, tag="o", bufs=4)
+            nc.tensor.matmul(out=pb[:], lhsT=ones[:], rhs=brow[:, h * 512 : (h + 1) * 512], start=True, stop=True)
+            nc.scalar.activation(out=b15[:, h * 512 : (h + 1) * 512], in_=pb[:], func=ACT.Copy, scale=INV_T)
+
+        nT = {}
+        lT = {}
+        tps = {}
+        pres = {}
+        codes = {}
+        scls = {}
+        obanks = {}
+        osbs = {}
+
+        def turn_noise(j):
+            xn = psum.tile([P, 2, 2, P], F32, name="xn%d" % j, tag="tA")
+            for g in range(2):
+                transpose_words(xn[:, g], n_words[j][:, g])
+            nT[j] = keep.tile([P, 2, 2, P], F32, name="nT%d" % j)
+            if j % 2 == 0:
+                nc.vector.tensor_copy(out=nT[j][:], in_=xn[:])
+            else:
+                nc.scalar.copy(out=nT[j][:], in_=xn[:])
+
+        def turn_lr(j):
+            lT[j] = psum.tile([P, 2, 2, P], F32, name="lT%d" % j, tag="tB")
+            for g in range(2):
+                transpose_words(lT[j][:, g], l_words[j][:, g])
+
+        def scale_noise(j):
+            tp = work.tile([P, 4, 2, P], F32, name="tp%d" % j, tag="tp")
+            tps[j] = tp
+            src = nT[j][:].bitcast(BF16).rearrange("p g u (r e) -> p g u r e", e=2)
+            for bl in range(GB):
+                b = GB * j + bl
+                rr = slice(16 * bl, 16 * bl + 16)
+                for t in range(4):
+                    nc.scalar.activation(
+                        out=tp[:, t, :, rr],
+                        in_=src[:, :, t // 2, rr, t % 2],
+                        func=ACT.Identity,
+                        bias=fg[:, b, t : t + 1],
+                        scale=std[:, t, b : b + 1],
+                    )
+
+        def add_lr(j):
+            pre = work.tile([P, 2, P, 4], BF16, name="pre%d" % j, tag="pre", align_bytes=64)
+            pres[j] = pre
+            a = lT[j][:].bitcast(BF16).rearrange("p g u (r e) -> p g r u e", e=2)
+            c = tps[j][:].rearrange("p (u e) g r -> p g r u e", e=2)
+            o = pre[:].rearrange("p g r (u e) -> p g r u e", e=2)
+            for g in range(2):
+                nc.vector.tensor_tensor(out=o[:, g], in0=a[:, g], in1=c[:, g], op=ALU.add)
+
+        def quantize(j):
+            codes[j] = work.tile([P, 2 * P], U32, name="codes%d" % j, tag="codes", align_bytes=64)
+            scls[j] = work.tile([P, 2 * P], U8, name="scl%d" % j, tag="scl", align_bytes=64)
+            nc.vector.quantize_mx(
+                out=codes[j][:].bitcast(FP8X4), scales=scls[j][:], in_=pres[j][:].rearrange("p g r t -> p (g r t)")
+            )
+
+        def multiply(j):
+            for g in range(2):
+                rows = slice(g * P, (g + 1) * P)
+                for h in range(2):
+                    cols = slice(h * 512, (h + 1) * 512)
+                    ob = psum.tile([P, 512], F32, name="ob%d_%d%d" % (j, g, h), tag="o", bufs=4)
+                    obanks[(j, g, h)] = ob
+                    nc.tensor.matmul_mx(
+                        out=ob[:],
+                        lhsT=codes[j][:, rows].bitcast(FP8X4),
+                        lhsT_scale=scls[j][:, rows],
+                        rhs=wc_codes[:, cols].bitcast(FP8X4),
+                        rhs_scale=wc_scl[:, cols],
+                        start=True,
+                        stop=True,
+                    )
+
+        def empty(j, g, h):
+            if (g, h) == (0, 0):
+                osbs[j] = work.tile([P, 2, C], F32, name="osb%d" % j, tag="osb")
+            cols = slice(h * 512, (h + 1) * 512)
+            dst = osbs[j][:, g, cols]
+            if j == NG - 1:
+                on_scalar = (g, h) == (0, 0)
+            else:
+                on_scalar = (g, h) == (1, 1) or ((g, h) == (0, 1) and j % 2 == 1)
+            if on_scalar:
+                nc.scalar.activation(out=dst, in_=obanks[(j, g, h)][:], func=ACT.Copy, scale=INV_T)
+                nc.gpsimd.tensor_tensor(out=dst, in0=dst, in1=b15[:, cols], op=ALU.add)
+            else:
+                nc.vector.scalar_tensor_tensor(
+                    out=dst, in0=obanks[(j, g, h)][:], scalar=INV_T, in1=b15[:, cols], op0=ALU.mult, op1=ALU.add
+                )
+
+        def store(j):
+            nc.sync.dma_start(out=o_rows[:, j], in_=osbs[j][:])
+
+        def store_half(j, g):
+            nc.sync.dma_start(out=o_rows[:, j, g], in_=osbs[j][:, g])
+
+        for j in range(HEAD_NOISE):
+            turn_noise(j)
+        turn_lr(0)
+        turn_lr(1)
+        scale_noise(0)
+        for j in range(NG + 1):
+            if j + 1 < NG:
+                scale_noise(j + 1)
+            if j < NG:
+                add_lr(j)
+            if j >= 1:
+                empty(j - 1, 0, 0)
+            if j < NG:
+                quantize(j)
+            if j + 2 < NG:
+                turn_lr(j + 2)
+            if j + HEAD_NOISE < NG:
+                turn_noise(j + HEAD_NOISE)
+            if j >= 1:
+                empty(j - 1, 0, 1)
+                if j == NG:
+                    store_half(j - 1, 0)
+                empty(j - 1, 1, 0)
+                empty(j - 1, 1, 1)
+                if j == NG:
+                    store_half(j - 1, 1)
+                else:
+                    store(j - 1)
+            if j < NG:
+                multiply(j)

@@ -18,8 +18,11 @@ ZBANK = F32
 NG = 16
 GB = 8
 INV_T = 1.0 / 1.5
-LOADS = (("n", 0, 2), ("n", 2, 2), ("w", 0, 0), ("l", 0, 2), ("n", 4, 4), ("l", 2, 2), ("n", 8, 4), ("l", 4, 4), ("n", 12, 4), ("l", 8, 4), ("l", 12, 4))
-HEAD_NOISE = 8
+LOADS = (("n", 0, 2), ("w", 0, 0), ("n", 2, 2), ("l", 0, 2), ("n", 4, 4), ("l", 2, 2), ("n", 8, 4), ("l", 4, 4), ("n", 12, 4), ("l", 8, 4), ("l", 12, 4))
+LOOP_NOISE = 8
+WARM_START = 4
+WARM_RUN = 2
+CUTS = (11, 21)
 
 
 def tile_hetxlhead_pa_kernel(tc, features, W_diag, b_diag, W_cls, b_cls, noise_diag, lr_samples, out):
@@ -28,10 +31,21 @@ def tile_hetxlhead_pa_kernel(tc, features, W_diag, b_diag, W_cls, b_cls, noise_d
         keep = ctx.enter_context(tc.tile_pool(name="keep", bufs=1))
         work = ctx.enter_context(tc.tile_pool(name="work", bufs=3))
         psum = ctx.enter_context(tc.psum_pool(name="psum", bufs=2))
+        ctx.enter_context(tc.manual_schedule())
 
         n_rows = noise_diag.rearrange("b s d -> (b s) d").rearrange("(j r g) d -> r j g d", r=P, g=2)
         l_rows = lr_samples.rearrange("b s d -> (b s) d").rearrange("(j r g) d -> r j g d", r=P, g=2)
         o_rows = out.rearrange("b s c -> (b s) c").rearrange("(j r g) c -> r j g c", r=P, g=2)
+
+        ident = keep.tile([P, P], F32, name="ident")
+        make_identity(nc, ident[:])
+        brow = keep.tile([P, C], BF16, name="brow")
+        nc.gpsimd.memset(brow[:], 0.0)
+        ones = keep.tile([P, P], BF16, name="ones")
+        nc.gpsimd.memset(ones[:], 1.0)
+        warm_in = keep.tile([P, 2], F32, name="warm_in")
+        nc.vector.memset(warm_in[:], 0.0)
+        nc.scalar.activation(out=warm_in[:, 1:2], in_=warm_in[:, 0:1], func=ACT.Exp)
 
         f_raw = keep.tile([P, D], BF16, name="f_raw")
         nc.sync.dma_start(out=f_raw[:], in_=features)
@@ -43,11 +57,7 @@ def tile_hetxlhead_pa_kernel(tc, features, W_diag, b_diag, W_cls, b_cls, noise_d
             wd_raw.append(wd_half)
         bd = keep.tile([P, 4], BF16, name="bd")
         nc.sync.dma_start(out=bd[:], in_=b_diag.rearrange("(p t) -> p t", t=4))
-
-        brow = keep.tile([P, C], BF16, name="brow")
-        nc.gpsimd.memset(brow[:], 0.0)
         wc_raw = keep.tile([P, 8, D], BF16, name="wc_raw")
-
         n_words = {}
         l_words = {}
         for li, (what, j0, n) in enumerate(LOADS):
@@ -64,31 +74,43 @@ def tile_hetxlhead_pa_kernel(tc, features, W_diag, b_diag, W_cls, b_cls, noise_d
                     else:
                         l_words[j0 + i] = raw[:, i].bitcast(F32)
 
-        ident = keep.tile([P, P], F32, name="ident")
-        make_identity(nc, ident[:])
-        ones = keep.tile([P, P], BF16, name="ones")
-        nc.gpsimd.memset(ones[:], 1.0)
-        warm = keep.tile([P, 2], F32, name="warm")
-        nc.vector.memset(warm[:], 0.0)
-        nc.scalar.activation(out=warm[:, 1:2], in_=warm[:, 0:1], func=ACT.Exp)
+        dummy = psum.tile([P, P], F32, name="dummy", tag="dm", bufs=1)
+
+        def warm(n):
+            for i in range(n):
+                nc.tensor.matmul(out=dummy[:], lhsT=ident[:], rhs=ident[:], start=True, stop=True)
 
         def transpose_words(dst, words):
             for u in range(2):
                 nc.tensor.transpose(out=dst[:, u, :], in_=words[:, u : 256 : 2], identity=ident[:])
 
-        xf = psum.tile([P, 2, 2, P], F32, name="xf", tag="tA")
+        nT = {}
+        xns = {}
+
+        def turn_noise(j, tag, bufs):
+            xns[j] = psum.tile([P, 2, 2, P], F32, name="xn%d" % j, tag=tag, bufs=bufs)
+            for g in range(2):
+                transpose_words(xns[j][:, g], n_words[j][:, g])
+
+        def copy_noise(j, on_scalar):
+            nT[j] = keep.tile([P, 2, 2, P], F32, name="nT%d" % j)
+            if on_scalar:
+                nc.scalar.copy(out=nT[j][:], in_=xns[j][:])
+            else:
+                nc.vector.tensor_copy(out=nT[j][:], in_=xns[j][:])
+
+        warm(WARM_START)
+        xf = psum.tile([P, 2, 2, P], F32, name="xf", tag="xn", bufs=1)
         transpose_words(xf[:, 0], f_raw[:].bitcast(F32))
         fg = keep.tile([P, B, 4], BF16, name="fg", align_bytes=64)
         nc.vector.tensor_copy(out=fg[:].bitcast(F32), in_=xf[:, 0].rearrange("p u b -> p b u"))
         f_codes = keep.tile([P, B], U32, name="f_codes", align_bytes=64)
         f_scl = keep.tile([P, B], U8, name="f_scl", align_bytes=64)
-
-        nc.vector.quantize_mx(out=f_codes[:].bitcast(FP8X4), scales=f_scl[:], in_=fg[:].rearrange("p b t -> p (b t)"))
         wd_codes = keep.tile([P, 4 * P], U32, name="wd_codes", align_bytes=64)
         wd_scl = keep.tile([P, 4 * P], U8, name="wd_scl", align_bytes=64)
         wdg = []
         for i in range(2):
-            xw = psum.tile([P, 2, 2, P], F32, name="xw%d" % i, tag="tB")
+            xw = psum.tile([P, 2, 2, P], F32, name="xw%d" % i, tag="lT")
             wd_words = wd_raw[i][:].bitcast(F32)
             for a in range(2):
                 transpose_words(xw[:, a], wd_words[:, a])
@@ -97,6 +119,9 @@ def tile_hetxlhead_pa_kernel(tc, features, W_diag, b_diag, W_cls, b_cls, noise_d
             src = xw[:].rearrange("p a u m -> p a m u")
             if i == 0:
                 nc.vector.tensor_copy(out=wdg_half[:].bitcast(F32), in_=src)
+                nc.vector.quantize_mx(
+                    out=f_codes[:].bitcast(FP8X4), scales=f_scl[:], in_=fg[:].rearrange("p b t -> p (b t)")
+                )
             else:
                 nc.scalar.copy(out=wdg_half[:].bitcast(F32), in_=src)
         for i in range(2):
@@ -104,8 +129,13 @@ def tile_hetxlhead_pa_kernel(tc, features, W_diag, b_diag, W_cls, b_cls, noise_d
             nc.vector.quantize_mx(
                 out=wd_codes[:, cols].bitcast(FP8X4), scales=wd_scl[:, cols], in_=wdg[i][:].rearrange("p t m k -> p (t m k)")
             )
+        warm(WARM_RUN)
+        for j in range(2):
+            turn_noise(j, "o", 4)
+            copy_noise(j, True)
+        warm(WARM_RUN)
 
-        zt = psum.tile([P, 4, P], ZBANK, name="zt", tag="tA")
+        zt = psum.tile([P, 4, P], ZBANK, name="zt", tag="xn", bufs=1)
         for t in range(4):
             cols = slice(t * P, (t + 1) * P)
             nc.tensor.matmul_mx(
@@ -128,7 +158,8 @@ def tile_hetxlhead_pa_kernel(tc, features, W_diag, b_diag, W_cls, b_cls, noise_d
         nc.vector.tensor_scalar(out=vr[:], in0=v[:], scalar1=0.0, scalar2=1e-3, op0=ALU.max, op1=ALU.add)
         vl = keep.tile([P, 4, B], F32, name="vl")
         std = keep.tile([P, 4, B], F32, name="std")
-        for b0, b1 in ((0, 32), (32, B)):
+
+        def finish_std(b0, b1):
             nc.scalar.activation(out=vl[:, :, b0:b1], in_=ve[:, :, b0:b1], func=ACT.Ln, bias=1.0)
             nc.vector.tensor_tensor(out=std[:, :, b0:b1], in0=vr[:, :, b0:b1], in1=vl[:, :, b0:b1], op=ALU.add)
 
@@ -140,12 +171,12 @@ def tile_hetxlhead_pa_kernel(tc, features, W_diag, b_diag, W_cls, b_cls, noise_d
             xc = psum.tile([P, 2, 2, P], F32, name="xc%d" % i, tag="o", bufs=4)
             for a in range(2):
                 transpose_words(xc[:, a], wc_words[:, 2 * i + a])
-            dst = wcg[:, 2 * i : 2 * i + 2].bitcast(F32)
-            src = xc[:].rearrange("p a u m -> p a m u")
-            if i % 2 == 0:
-                nc.vector.tensor_copy(out=dst, in_=src)
-            else:
-                nc.scalar.copy(out=dst, in_=src)
+            if i % 2 == 1:
+                warm(WARM_RUN)
+            nc.vector.tensor_copy(out=wcg[:, 2 * i : 2 * i + 2].bitcast(F32), in_=xc[:].rearrange("p a u m -> p a m u"))
+            if i == 1:
+                finish_std(0, 32)
+        finish_std(32, B)
         for h in range(2):
             nc.vector.quantize_mx(
                 out=wc_codes[:, h * 512 : (h + 1) * 512].bitcast(FP8X4),
@@ -156,9 +187,8 @@ def tile_hetxlhead_pa_kernel(tc, features, W_diag, b_diag, W_cls, b_cls, noise_d
         for h in range(2):
             pb = psum.tile([P, 512], F32, name="pb%d" % h, tag="o", bufs=4)
             nc.tensor.matmul(out=pb[:], lhsT=ones[:], rhs=brow[:, h * 512 : (h + 1) * 512], start=True, stop=True)
-            nc.scalar.activation(out=b15[:, h * 512 : (h + 1) * 512], in_=pb[:], func=ACT.Copy, scale=INV_T)
+            nc.vector.tensor_scalar_mul(out=b15[:, h * 512 : (h + 1) * 512], in0=pb[:], scalar1=INV_T)
 
-        nT = {}
         lT = {}
         tps = {}
         pres = {}
@@ -167,36 +197,27 @@ def tile_hetxlhead_pa_kernel(tc, features, W_diag, b_diag, W_cls, b_cls, noise_d
         obanks = {}
         osbs = {}
 
-        def turn_noise(j):
-            xn = psum.tile([P, 2, 2, P], F32, name="xn%d" % j, tag="tA")
-            for g in range(2):
-                transpose_words(xn[:, g], n_words[j][:, g])
-            nT[j] = keep.tile([P, 2, 2, P], F32, name="nT%d" % j)
-            if j % 2 == 0:
-                nc.vector.tensor_copy(out=nT[j][:], in_=xn[:])
-            else:
-                nc.scalar.copy(out=nT[j][:], in_=xn[:])
-
         def turn_lr(j):
-            lT[j] = psum.tile([P, 2, 2, P], F32, name="lT%d" % j, tag="tB")
+            lT[j] = psum.tile([P, 2, 2, P], F32, name="lT%d" % j, tag="lT")
             for g in range(2):
                 transpose_words(lT[j][:, g], l_words[j][:, g])
 
-        def scale_noise(j):
-            tp = work.tile([P, 4, 2, P], F32, name="tp%d" % j, tag="tp")
-            tps[j] = tp
+        def scale_noise(j, first, last):
+            if first == 0:
+                tps[j] = work.tile([P, 4, 2, P], F32, name="tp%d" % j, tag="tp")
             src = nT[j][:].bitcast(BF16).rearrange("p g u (r e) -> p g u r e", e=2)
-            for bl in range(GB):
+            for i in range(first, last):
+                bl = i // 4
+                t = i % 4
                 b = GB * j + bl
                 rr = slice(16 * bl, 16 * bl + 16)
-                for t in range(4):
-                    nc.scalar.activation(
-                        out=tp[:, t, :, rr],
-                        in_=src[:, :, t // 2, rr, t % 2],
-                        func=ACT.Identity,
-                        bias=fg[:, b, t : t + 1],
-                        scale=std[:, t, b : b + 1],
-                    )
+                nc.scalar.activation(
+                    out=tps[j][:, t, :, rr],
+                    in_=src[:, :, t // 2, rr, t % 2],
+                    func=ACT.Identity,
+                    bias=fg[:, b, t : t + 1],
+                    scale=std[:, t, b : b + 1],
+                )
 
         def add_lr(j):
             pre = work.tile([P, 2, P, 4], BF16, name="pre%d" % j, tag="pre", align_bytes=64)
@@ -214,73 +235,101 @@ def tile_hetxlhead_pa_kernel(tc, features, W_diag, b_diag, W_cls, b_cls, noise_d
                 out=codes[j][:].bitcast(FP8X4), scales=scls[j][:], in_=pres[j][:].rearrange("p g r t -> p (g r t)")
             )
 
-        def multiply(j):
-            for g in range(2):
-                rows = slice(g * P, (g + 1) * P)
-                for h in range(2):
-                    cols = slice(h * 512, (h + 1) * 512)
-                    ob = psum.tile([P, 512], F32, name="ob%d_%d%d" % (j, g, h), tag="o", bufs=4)
-                    obanks[(j, g, h)] = ob
-                    nc.tensor.matmul_mx(
-                        out=ob[:],
-                        lhsT=codes[j][:, rows].bitcast(FP8X4),
-                        lhsT_scale=scls[j][:, rows],
-                        rhs=wc_codes[:, cols].bitcast(FP8X4),
-                        rhs_scale=wc_scl[:, cols],
-                        start=True,
-                        stop=True,
-                    )
-
-        def empty(j, g, h):
-            if (g, h) == (0, 0):
-                osbs[j] = work.tile([P, 2, C], F32, name="osb%d" % j, tag="osb")
+        def multiply(j, k):
+            g = k // 2
+            h = k % 2
+            rows = slice(g * P, (g + 1) * P)
             cols = slice(h * 512, (h + 1) * 512)
-            dst = osbs[j][:, g, cols]
-            if j == NG - 1:
-                on_scalar = (g, h) == (0, 0)
-            else:
-                on_scalar = (g, h) == (1, 1) or ((g, h) == (0, 1) and j % 2 == 1)
+            ob = psum.tile([P, 512], F32, name="ob%d_%d" % (j, k), tag="o", bufs=4)
+            obanks[(j, k)] = ob
+            nc.tensor.matmul_mx(
+                out=ob[:],
+                lhsT=codes[j][:, rows].bitcast(FP8X4),
+                lhsT_scale=scls[j][:, rows],
+                rhs=wc_codes[:, cols].bitcast(FP8X4),
+                rhs_scale=wc_scl[:, cols],
+                start=True,
+                stop=True,
+            )
+
+        def empty(j, k, on_scalar):
+            if j not in osbs:
+                osbs[j] = work.tile([P, 2, C], F32, name="osb%d" % j, tag="osb")
+            cols = slice((k % 2) * 512, (k % 2 + 1) * 512)
+            dst = osbs[j][:, k // 2, cols]
             if on_scalar:
-                nc.scalar.activation(out=dst, in_=obanks[(j, g, h)][:], func=ACT.Copy, scale=INV_T)
+                nc.scalar.activation(out=dst, in_=obanks[(j, k)][:], func=ACT.Copy, scale=INV_T)
                 nc.gpsimd.tensor_tensor(out=dst, in0=dst, in1=b15[:, cols], op=ALU.add)
             else:
                 nc.vector.scalar_tensor_tensor(
-                    out=dst, in0=obanks[(j, g, h)][:], scalar=INV_T, in1=b15[:, cols], op0=ALU.mult, op1=ALU.add
+                    out=dst, in0=obanks[(j, k)][:], scalar=INV_T, in1=b15[:, cols], op0=ALU.mult, op1=ALU.add
                 )
 
-        def store(j):
-            nc.sync.dma_start(out=o_rows[:, j], in_=osbs[j][:])
+        for step in range(NG + 2):
+            jw = step
+            ja = step - 1
+            je = step - 2
+            do_w = jw < NG
+            do_a = 0 <= ja < NG
+            do_e = je >= 0
+            last = je == NG - 1
+            jn = step + 2
+            loop_noise = LOOP_NOISE <= jn < NG
+            scalar_takes = (0,) if last else ((1, 3) if (je % 2 == 1 or step >= NG) else (3,))
 
-        def store_half(j, g):
-            nc.sync.dma_start(out=o_rows[:, j, g], in_=osbs[j][:, g])
+            if do_w:
+                turn_lr(jw)
+            if loop_noise:
+                turn_noise(jn, "xn", 1)
+            if step == 0:
+                for j in (2, 3):
+                    turn_noise(j, "o", 4)
+                warm(WARM_RUN)
+                for j in (4, 5):
+                    turn_noise(j, "o", 4)
+            if step == 1:
+                for j in (6, 7):
+                    turn_noise(j, "o", 4)
+            if step < NG + 1:
+                warm(WARM_RUN)
 
-        for j in range(HEAD_NOISE):
-            turn_noise(j)
-        turn_lr(0)
-        turn_lr(1)
-        scale_noise(0)
-        for j in range(NG + 1):
-            if j + 1 < NG:
-                scale_noise(j + 1)
-            if j < NG:
-                add_lr(j)
-            if j >= 1:
-                empty(j - 1, 0, 0)
-            if j < NG:
-                quantize(j)
-            if j + 2 < NG:
-                turn_lr(j + 2)
-            if j + HEAD_NOISE < NG:
-                turn_noise(j + HEAD_NOISE)
-            if j >= 1:
-                empty(j - 1, 0, 1)
-                if j == NG:
-                    store_half(j - 1, 0)
-                empty(j - 1, 1, 0)
-                empty(j - 1, 1, 1)
-                if j == NG:
-                    store_half(j - 1, 1)
+            if do_w:
+                scale_noise(jw, 0, CUTS[0])
+            if step == 0:
+                for j in (2, 3, 4, 5):
+                    copy_noise(j, False)
+            if do_a:
+                add_lr(ja)
+            if step == 1:
+                copy_noise(6, False)
+            if do_e:
+                empty(je, 0, 0 in scalar_takes)
+            if do_a:
+                quantize(ja)
+                multiply(ja, 0)
+            if step == 1:
+                copy_noise(7, False)
+            if do_e:
+                empty(je, 1, 1 in scalar_takes)
+                if last:
+                    nc.sync.dma_start(out=o_rows[:, je, 0], in_=osbs[je][:, 0])
+            if do_a:
+                multiply(ja, 1)
+            if do_w:
+                scale_noise(jw, CUTS[0], CUTS[1])
+            if do_e:
+                empty(je, 3, 3 in scalar_takes)
+            if loop_noise:
+                copy_noise(jn, True)
+            if do_e:
+                empty(je, 2, 2 in scalar_takes)
+            if do_a:
+                multiply(ja, 2)
+                multiply(ja, 3)
+            if do_w:
+                scale_noise(jw, CUTS[1], 32)
+            if do_e:
+                if last:
+                    nc.sync.dma_start(out=o_rows[:, je, 1], in_=osbs[je][:, 1])
                 else:
-                    store(j - 1)
-            if j < NG:
-                multiply(j)
+                    nc.sync.dma_start(out=o_rows[:, je], in_=osbs[je][:])

from contextlib import ExitStack

import concourse.mybir as mybir
from concourse.masks import make_identity

F32 = mybir.dt.float32
BF16 = mybir.dt.bfloat16
U32 = mybir.dt.uint32
U8 = mybir.dt.uint8
FP8X4 = mybir.dt.float8_e4m3fn_x4
ALU = mybir.AluOpType
ACT = mybir.ActivationFunctionType

B, S, D, C = 128, 32, 512, 1024
P = 128
FLOPS = 2 * B * S * D * C + 2 * B * D * D
ZBANK = F32
NG = 16
GB = 8
INV_T = 1.0 / 1.5
LOADS = (("n", 0, 2), ("w", 0, 0), ("n", 2, 2), ("l", 0, 2), ("n", 4, 4), ("l", 2, 2), ("n", 8, 4), ("l", 4, 4), ("n", 12, 4), ("l", 8, 4), ("l", 12, 4))
LOOP_NOISE = 8
WARM_START = 4
WARM_RUN = 2
CUTS = (11, 21)


def tile_hetxlhead_pa_kernel(tc, features, W_diag, b_diag, W_cls, b_cls, noise_diag, lr_samples, out):
    nc = tc.nc
    with ExitStack() as ctx:
        keep = ctx.enter_context(tc.tile_pool(name="keep", bufs=1))
        work = ctx.enter_context(tc.tile_pool(name="work", bufs=3))
        psum = ctx.enter_context(tc.psum_pool(name="psum", bufs=2))
        ctx.enter_context(tc.manual_schedule())

        n_rows = noise_diag.rearrange("b s d -> (b s) d").rearrange("(j r g) d -> r j g d", r=P, g=2)
        l_rows = lr_samples.rearrange("b s d -> (b s) d").rearrange("(j r g) d -> r j g d", r=P, g=2)
        o_rows = out.rearrange("b s c -> (b s) c").rearrange("(j r g) c -> r j g c", r=P, g=2)

        ident = keep.tile([P, P], F32, name="ident")
        make_identity(nc, ident[:])
        brow = keep.tile([P, C], BF16, name="brow")
        nc.gpsimd.memset(brow[:], 0.0)
        ones = keep.tile([P, P], BF16, name="ones")
        nc.gpsimd.memset(ones[:], 1.0)
        warm_in = keep.tile([P, 2], F32, name="warm_in")
        nc.vector.memset(warm_in[:], 0.0)
        nc.scalar.activation(out=warm_in[:, 1:2], in_=warm_in[:, 0:1], func=ACT.Exp)

        f_raw = keep.tile([P, D], BF16, name="f_raw")
        nc.sync.dma_start(out=f_raw[:], in_=features)
        wd_rows = W_diag.rearrange("(m t) k -> m t k", t=4)
        wd_raw = []
        for i in range(2):
            wd_half = keep.tile([P, 2, D], BF16, name="wd_raw%d" % i)
            nc.sync.dma_start(out=wd_half[:], in_=wd_rows[:, 2 * i : 2 * i + 2])
            wd_raw.append(wd_half)
        bd = keep.tile([P, 4], BF16, name="bd")
        nc.sync.dma_start(out=bd[:], in_=b_diag.rearrange("(p t) -> p t", t=4))
        wc_raw = keep.tile([P, 8, D], BF16, name="wc_raw")
        n_words = {}
        l_words = {}
        for li, (what, j0, n) in enumerate(LOADS):
            if what == "w":
                nc.sync.dma_start(out=wc_raw[:], in_=W_cls.rearrange("(a p) d -> p a d", p=P))
                nc.sync.dma_start(out=brow[0:1, :], in_=b_cls.rearrange("(o c) -> o c", o=1))
            else:
                raw = keep.tile([P, n, 2, D], BF16, name="raw%d" % li)
                rows = n_rows if what == "n" else l_rows
                nc.sync.dma_start(out=raw[:], in_=rows[:, j0 : j0 + n])
                for i in range(n):
                    if what == "n":
                        n_words[j0 + i] = raw[:, i].bitcast(F32)
                    else:
                        l_words[j0 + i] = raw[:, i].bitcast(F32)

        dummy = psum.tile([P, P], F32, name="dummy", tag="dm", bufs=1)

        def warm(n):
            for i in range(n):
                nc.tensor.matmul(out=dummy[:], lhsT=ident[:], rhs=ident[:], start=True, stop=True)

        def transpose_words(dst, words):
            for u in range(2):
                nc.tensor.transpose(out=dst[:, u, :], in_=words[:, u : 256 : 2], identity=ident[:])

        nT = {}
        xns = {}

        def turn_noise(j, tag, bufs):
            xns[j] = psum.tile([P, 2, 2, P], F32, name="xn%d" % j, tag=tag, bufs=bufs)
            for g in range(2):
                transpose_words(xns[j][:, g], n_words[j][:, g])

        def copy_noise(j, on_scalar):
            nT[j] = keep.tile([P, 2, 2, P], F32, name="nT%d" % j)
            if on_scalar:
                nc.scalar.copy(out=nT[j][:], in_=xns[j][:])
            else:
                nc.vector.tensor_copy(out=nT[j][:], in_=xns[j][:])

        warm(WARM_START)
        xf = psum.tile([P, 2, 2, P], F32, name="xf", tag="xn", bufs=1)
        transpose_words(xf[:, 0], f_raw[:].bitcast(F32))
        fg = keep.tile([P, B, 4], BF16, name="fg", align_bytes=64)
        nc.vector.tensor_copy(out=fg[:].bitcast(F32), in_=xf[:, 0].rearrange("p u b -> p b u"))
        f_codes = keep.tile([P, B], U32, name="f_codes", align_bytes=64)
        f_scl = keep.tile([P, B], U8, name="f_scl", align_bytes=64)
        wd_codes = keep.tile([P, 4 * P], U32, name="wd_codes", align_bytes=64)
        wd_scl = keep.tile([P, 4 * P], U8, name="wd_scl", align_bytes=64)
        wdg = []
        for i in range(2):
            xw = psum.tile([P, 2, 2, P], F32, name="xw%d" % i, tag="lT")
            wd_words = wd_raw[i][:].bitcast(F32)
            for a in range(2):
                transpose_words(xw[:, a], wd_words[:, a])
            wdg_half = keep.tile([P, 2, P, 4], BF16, name="wdg%d" % i, align_bytes=64)
            wdg.append(wdg_half)
            src = xw[:].rearrange("p a u m -> p a m u")
            if i == 0:
                nc.vector.tensor_copy(out=wdg_half[:].bitcast(F32), in_=src)
                nc.vector.quantize_mx(
                    out=f_codes[:].bitcast(FP8X4), scales=f_scl[:], in_=fg[:].rearrange("p b t -> p (b t)")
                )
            else:
                nc.scalar.copy(out=wdg_half[:].bitcast(F32), in_=src)
        for i in range(2):
            cols = slice(2 * i * P, (2 * i + 2) * P)
            nc.vector.quantize_mx(
                out=wd_codes[:, cols].bitcast(FP8X4), scales=wd_scl[:, cols], in_=wdg[i][:].rearrange("p t m k -> p (t m k)")
            )
        warm(WARM_RUN)
        for j in range(2):
            turn_noise(j, "o", 4)
            copy_noise(j, True)
        warm(WARM_RUN)

        zt = psum.tile([P, 4, P], ZBANK, name="zt", tag="xn", bufs=1)
        for t in range(4):
            cols = slice(t * P, (t + 1) * P)
            nc.tensor.matmul_mx(
                out=zt[:, t, :],
                lhsT=wd_codes[:, cols].bitcast(FP8X4),
                lhsT_scale=wd_scl[:, cols],
                rhs=f_codes[:].bitcast(FP8X4),
                rhs_scale=f_scl[:],
                start=True,
                stop=True,
            )

        v = keep.tile([P, 4, B], F32, name="v")
        nc.vector.tensor_tensor(out=v[:], in0=zt[:], in1=bd[:].unsqueeze(2).to_broadcast([P, 4, B]), op=ALU.add)
        va = keep.tile([P, 4, B], F32, name="va")
        nc.scalar.activation(out=va[:], in_=v[:], func=ACT.Abs)
        ve = keep.tile([P, 4, B], F32, name="ve")
        nc.scalar.activation(out=ve[:], in_=va[:], func=ACT.Exp, scale=-1.0)
        vr = keep.tile([P, 4, B], F32, name="vr")
        nc.vector.tensor_scalar(out=vr[:], in0=v[:], scalar1=0.0, scalar2=1e-3, op0=ALU.max, op1=ALU.add)
        vl = keep.tile([P, 4, B], F32, name="vl")
        std = keep.tile([P, 4, B], F32, name="std")

        def finish_std(b0, b1):
            nc.scalar.activation(out=vl[:, :, b0:b1], in_=ve[:, :, b0:b1], func=ACT.Ln, bias=1.0)
            nc.vector.tensor_tensor(out=std[:, :, b0:b1], in0=vr[:, :, b0:b1], in1=vl[:, :, b0:b1], op=ALU.add)

        wc_words = wc_raw[:].bitcast(F32)
        wcg = keep.tile([P, 8, P, 4], BF16, name="wcg", align_bytes=64)
        wc_codes = keep.tile([P, C], U32, name="wc_codes", align_bytes=64)
        wc_scl = keep.tile([P, C], U8, name="wc_scl", align_bytes=64)
        for i in range(4):
            xc = psum.tile([P, 2, 2, P], F32, name="xc%d" % i, tag="o", bufs=4)
            for a in range(2):
                transpose_words(xc[:, a], wc_words[:, 2 * i + a])
            if i % 2 == 1:
                warm(WARM_RUN)
            nc.vector.tensor_copy(out=wcg[:, 2 * i : 2 * i + 2].bitcast(F32), in_=xc[:].rearrange("p a u m -> p a m u"))
            if i == 1:
                finish_std(0, 32)
        finish_std(32, B)
        for h in range(2):
            nc.vector.quantize_mx(
                out=wc_codes[:, h * 512 : (h + 1) * 512].bitcast(FP8X4),
                scales=wc_scl[:, h * 512 : (h + 1) * 512],
                in_=wcg[:, 4 * h : 4 * h + 4].rearrange("p a m k -> p (a m k)"),
            )
        b15 = keep.tile([P, C], F32, name="b15")
        for h in range(2):
            pb = psum.tile([P, 512], F32, name="pb%d" % h, tag="o", bufs=4)
            nc.tensor.matmul(out=pb[:], lhsT=ones[:], rhs=brow[:, h * 512 : (h + 1) * 512], start=True, stop=True)
            nc.vector.tensor_scalar_mul(out=b15[:, h * 512 : (h + 1) * 512], in0=pb[:], scalar1=INV_T)

        lT = {}
        tps = {}
        pres = {}
        codes = {}
        scls = {}
        obanks = {}
        osbs = {}

        def turn_lr(j):
            lT[j] = psum.tile([P, 2, 2, P], F32, name="lT%d" % j, tag="lT")
            for g in range(2):
                transpose_words(lT[j][:, g], l_words[j][:, g])

        def scale_noise(j, first, last):
            if first == 0:
                tps[j] = work.tile([P, 4, 2, P], F32, name="tp%d" % j, tag="tp")
            src = nT[j][:].bitcast(BF16).rearrange("p g u (r e) -> p g u r e", e=2)
            for i in range(first, last):
                bl = i // 4
                t = i % 4
                b = GB * j + bl
                rr = slice(16 * bl, 16 * bl + 16)
                nc.scalar.activation(
                    out=tps[j][:, t, :, rr],
                    in_=src[:, :, t // 2, rr, t % 2],
                    func=ACT.Identity,
                    bias=fg[:, b, t : t + 1],
                    scale=std[:, t, b : b + 1],
                )

        def add_lr(j):
            pre = work.tile([P, 2, P, 4], BF16, name="pre%d" % j, tag="pre", align_bytes=64)
            pres[j] = pre
            a = lT[j][:].bitcast(BF16).rearrange("p g u (r e) -> p g r u e", e=2)
            c = tps[j][:].rearrange("p (u e) g r -> p g r u e", e=2)
            o = pre[:].rearrange("p g r (u e) -> p g r u e", e=2)
            for g in range(2):
                nc.vector.tensor_tensor(out=o[:, g], in0=a[:, g], in1=c[:, g], op=ALU.add)

        def quantize(j):
            codes[j] = work.tile([P, 2 * P], U32, name="codes%d" % j, tag="codes", align_bytes=64)
            scls[j] = work.tile([P, 2 * P], U8, name="scl%d" % j, tag="scl", align_bytes=64)
            nc.vector.quantize_mx(
                out=codes[j][:].bitcast(FP8X4), scales=scls[j][:], in_=pres[j][:].rearrange("p g r t -> p (g r t)")
            )

        def multiply(j, k):
            g = k // 2
            h = k % 2
            rows = slice(g * P, (g + 1) * P)
            cols = slice(h * 512, (h + 1) * 512)
            ob = psum.tile([P, 512], F32, name="ob%d_%d" % (j, k), tag="o", bufs=4)
            obanks[(j, k)] = ob
            nc.tensor.matmul_mx(
                out=ob[:],
                lhsT=codes[j][:, rows].bitcast(FP8X4),
                lhsT_scale=scls[j][:, rows],
                rhs=wc_codes[:, cols].bitcast(FP8X4),
                rhs_scale=wc_scl[:, cols],
                start=True,
                stop=True,
            )

        def empty(j, k, on_scalar):
            if j not in osbs:
                osbs[j] = work.tile([P, 2, C], F32, name="osb%d" % j, tag="osb")
            cols = slice((k % 2) * 512, (k % 2 + 1) * 512)
            dst = osbs[j][:, k // 2, cols]
            if on_scalar:
                nc.scalar.activation(out=dst, in_=obanks[(j, k)][:], func=ACT.Copy, scale=INV_T)
                nc.gpsimd.tensor_tensor(out=dst, in0=dst, in1=b15[:, cols], op=ALU.add)
            else:
                nc.vector.scalar_tensor_tensor(
                    out=dst, in0=obanks[(j, k)][:], scalar=INV_T, in1=b15[:, cols], op0=ALU.mult, op1=ALU.add
                )

        for step in range(NG + 2):
            jw = step
            ja = step - 1
            je = step - 2
            do_w = jw < NG
            do_a = 0 <= ja < NG
            do_e = je >= 0
            last = je == NG - 1
            jn = step + 2
            loop_noise = LOOP_NOISE <= jn < NG
            scalar_takes = (0,) if last else ((1, 3) if (je % 2 == 1 or step >= NG) else (3,))

            if do_w:
                turn_lr(jw)
            if loop_noise:
                turn_noise(jn, "xn", 1)
            if step == 0:
                for j in (2, 3):
                    turn_noise(j, "o", 4)
                warm(WARM_RUN)
                for j in (4, 5):
                    turn_noise(j, "o", 4)
            if step == 1:
                for j in (6, 7):
                    turn_noise(j, "o", 4)
            if step < NG + 1:
                warm(WARM_RUN)

            if do_w:
                scale_noise(jw, 0, CUTS[0])
            if step == 0:
                for j in (2, 3, 4, 5):
                    copy_noise(j, False)
            if do_a:
                add_lr(ja)
            if step == 1:
                copy_noise(6, False)
            if do_e:
                empty(je, 0, 0 in scalar_takes)
            if do_a:
                quantize(ja)
                multiply(ja, 0)
            if step == 1:
                copy_noise(7, False)
            if do_e:
                empty(je, 1, 1 in scalar_takes)
                if last:
                    nc.sync.dma_start(out=o_rows[:, je, 0], in_=osbs[je][:, 0])
            if do_a:
                multiply(ja, 1)
            if do_w:
                scale_noise(jw, CUTS[0], CUTS[1])
            if do_e:
                empty(je, 3, 3 in scalar_takes)
            if loop_noise:
                copy_noise(jn, True)
            if do_e:
                empty(je, 2, 2 in scalar_takes)
            if do_a:
                multiply(ja, 2)
                multiply(ja, 3)
            if do_w:
                scale_noise(jw, CUTS[1], 32)
            if do_e:
                if last:
                    nc.sync.dma_start(out=o_rows[:, je, 1], in_=osbs[je][:, 1])
                else:
                    nc.sync.dma_start(out=o_rows[:, je], in_=osbs[je][:])
